import numpy as np
import ml_dtypes


def mxq(x, axis, fmt="e4m3"):
    dtype, down = {"e4m3": (ml_dtypes.float8_e4m3fn, 7), "e5m2": (ml_dtypes.float8_e5m2, 14)}[fmt]
    v = np.moveaxis(np.asarray(x, np.float32).astype(ml_dtypes.bfloat16).astype(np.float64), axis, -1)
    blocks = v.reshape(v.shape[:-1] + (-1, 32))
    amax = np.abs(blocks).max(-1, keepdims=True)
    byte = np.maximum(np.where(amax > 0, np.frexp(amax)[1] - 1 + 127, 0) - down, 1)
    scale = np.exp2(byte - 127.0)
    codes = (blocks / scale).astype(np.float32).astype(dtype).astype(np.float64)
    return np.moveaxis((codes * scale).reshape(v.shape), -1, axis)


WIDE = False


def mx_kscale(k):
    if not WIDE:
        return np.ones(k)
    levels = np.array([10, -10, 5, -5, 0])
    a = np.random.permutation(np.resize(levels, k // 512 * 4)).reshape(k // 512, 4)
    idx = np.arange(k)
    return np.exp2(a[idx // 512, idx % 128 // 32])


BF16 = ml_dtypes.bfloat16


def bf(x):
    return np.asarray(x, np.float32).astype(BF16)


def f64(x):
    return np.asarray(x).astype(np.float64)


C, P, B, D = 7, 512, 2, 256
N = C * P
ID = C // 2


def laplacian_with_self_loop(adj):
    a = adj + np.eye(adj.shape[0])
    d_inv_sqrt = 1.0 / np.sqrt(a.sum(axis=1))
    return d_inv_sqrt[:, None] * a * d_inv_sqrt[None, :]


def setup_inputs():
    s = mx_kscale(P)
    sp = s / s.min()
    r = np.exp2(np.random.uniform(-1.0, 1.0, N))
    adj = np.random.uniform(0.0, 1.0, (N, N)) * r[:, None] * np.tile(sp, C)[None, :]
    x = np.random.standard_normal((P, B * D)) * (0.15 * N * sp.mean() / np.sqrt(P / 3.0)) / sp[:, None]
    return {"globalAdj": bf(adj), "inputs": bf(x), "batch_size": B, "output_dim": D, "id": ID}


def reference(globalAdj, inputs, batch_size, output_dim, id):
    lap = laplacian_with_self_loop(f64(globalAdj))
    col = lap[:, id * P:(id + 1) * P]
    out = mxq(col, 1, "e4m3") @ mxq(f64(inputs), 0, "e4m3")
    out = out.reshape(N, batch_size, output_dim)
    return out.transpose(1, 0, 2)

@@ -1,0 +1,181 @@
+from contextlib import ExitStack
+
+import concourse.mybir as mybir
+from concourse.masks import make_identity
+
+FLOPS = 2 * 3584 * 512 * 512
+
+BF16 = mybir.dt.bfloat16
+F32 = mybir.dt.float32
+U32 = mybir.dt.uint32
+U8 = mybir.dt.uint8
+FP8X4 = mybir.dt.float8_e4m3fn_x4
+ALU = mybir.AluOpType
+ACT = mybir.ActivationFunctionType
+
+P = 128
+N = 3584
+K = 512
+HV = 1312
+A_BUFS = 10
+
+
+def tile_gcn_kernel(tc, adj, feats, batch_size, output_dim, client, out):
+    nc = tc.nc
+    col0 = client * K
+    cs = N - 2 * HV
+    units = [(col0, 4), (0, 4), (512, 4), (1024, 4), (2048, 4), (2560, 4), (3072, 2), (3328, 1), (3456, 1)]
+    pieces = []
+    for u, (base, rows) in enumerate(units):
+        for r0 in range(0, rows, 2):
+            pieces.append((u, r0, min(2, rows - r0)))
+
+    with ExitStack() as ctx:
+        const = ctx.enter_context(tc.tile_pool(name="const", bufs=1))
+        apool = ctx.enter_context(tc.tile_pool(name="apool", bufs=A_BUFS))
+        work = ctx.enter_context(tc.tile_pool(name="work", bufs=2))
+        small = ctx.enter_context(tc.tile_pool(name="small", bufs=4))
+        ypool = ctx.enter_context(tc.tile_pool(name="ypool", bufs=3))
+        ps_t = ctx.enter_context(tc.psum_pool(name="ps_t", bufs=3))
+        ps_y = ctx.enter_context(tc.psum_pool(name="ps_y", bufs=4))
+        ps_d = ctx.enter_context(tc.psum_pool(name="ps_d", bufs=1))
+
+        a_tiles = {}
+
+        def issue_load(i):
+            u, r0, nr = pieces[i]
+            base, rows = units[u]
+            a_t = apool.tile([P, 2, N], BF16, name="a_t")
+            src = adj[base : base + P * rows, :].rearrange("(p r) c -> p r c", r=rows)
+            if u == 0:
+                for j in range(nr):
+                    nc.sync.dma_start(out=a_t[:, j : j + 1, :], in_=src[:, r0 + j : r0 + j + 1, :])
+            else:
+                nc.sync.dma_start(out=a_t[:, 0:nr, :], in_=src[:, r0 : r0 + nr, :])
+            a_tiles[i] = a_t
+
+        n_loaded = min(A_BUFS, len(pieces))
+        for i in range(2):
+            issue_load(i)
+        x_raw = work.tile([P, 4, K], BF16, name="x_raw", tag="colb")
+        nc.sync.dma_start(out=x_raw[:], in_=feats.rearrange("(t q) f -> q t f", q=P))
+        for i in range(2, n_loaded):
+            issue_load(i)
+
+        ident_b = const.tile([P, P], BF16, name="ident_b")
+        make_identity(nc, ident_b[:])
+        ident_f = const.tile([P, P], F32, name="ident_f")
+        make_identity(nc, ident_f[:])
+        epad = const.tile([P, K + 4], BF16, name="epad")
+        nc.gpsimd.memset(epad[:], 0.0)
+        nc.gpsimd.tensor_copy(
+            out=epad[:, 3 : 3 + K].rearrange("p (q r) -> p q r", r=4)[:, :, 0], in_=ident_b[:]
+        )
+
+        x_codes = const.tile([P, K], U32, name="x_codes", align_bytes=64)
+        x_scales = const.tile([P, K], U8, name="x_scales", align_bytes=64)
+        djb = const.tile([P, P, 4], F32, name="djb")
+        dj_flat = djb[:].rearrange("m n r -> m (n r)")
+
+        for u, (base, rows) in enumerate(units):
+            mine = [i for i in range(len(pieces)) if pieces[i][0] == u]
+            s_v = small.tile([P, 4], F32, name="s_v")
+            s_s = small.tile([P, 4], F32, name="s_s")
+            for i in mine:
+                r0, nr = pieces[i][1], pieces[i][2]
+                for j in range(nr):
+                    r = r0 + j
+                    junk_v = work.tile([P, HV], F32, name="junk_v")
+                    nc.vector.scalar_tensor_tensor(
+                        out=junk_v[:],
+                        in0=a_tiles[i][:, j, 0:HV],
+                        scalar=1.0,
+                        in1=a_tiles[i][:, j, HV : 2 * HV],
+                        op0=ALU.mult,
+                        op1=ALU.add,
+                        accum_out=s_v[:, r : r + 1],
+                    )
+                    junk_s = work.tile([P, cs], BF16, name="junk_s")
+                    nc.scalar.activation(
+                        out=junk_s[:],
+                        in_=a_tiles[i][:, j, 2 * HV : N],
+                        func=ACT.Copy,
+                        accum_out=s_s[:, r : r + 1],
+                    )
+            deg = small.tile([P, 4], F32, name="deg")
+            nc.vector.scalar_tensor_tensor(
+                out=deg[:, 0:rows], in0=s_v[:, 0:rows], scalar=1.0, in1=s_s[:, 0:rows], op0=ALU.add, op1=ALU.add
+            )
+            root = small.tile([P, 4], F32, name="root")
+            nc.scalar.activation(out=root[:, 0:rows], in_=deg[:, 0:rows], func=ACT.Sqrt)
+            dinv = small.tile([P, 4], F32, name="dinv")
+            nc.vector.reciprocal(out=dinv[:, 0:rows], in_=root[:, 0:rows])
+
+            if u == 0:
+                x_grp = work.tile([P, K, 4], BF16, name="x_grp", tag="grp", align_bytes=64)
+                nc.vector.tensor_copy(out=x_grp[:], in_=x_raw[:].rearrange("q t f -> q f t"))
+                spread = const.tile([P, 4, P], F32, name="spread")
+                nc.vector.tensor_copy(out=spread[:], in_=dinv[:].unsqueeze(2).to_broadcast([P, 4, P]))
+                dj_ps = ps_d.tile([P, 4, P], F32, name="dj_ps")
+                for r in range(4):
+                    nc.tensor.transpose(dj_ps[:, r, :], spread[:, r, :], ident_f[:])
+                nc.vector.tensor_copy(out=djb[:], in_=dj_ps[:].rearrange("m r n -> m n r"))
+                nc.vector.quantize_mx(
+                    out=x_codes[:].bitcast(FP8X4), scales=x_scales[:], in_=x_grp[:].rearrange("q f t -> q (f t)")
+                )
+
+            colb = work.tile([P, 4, K], BF16, name="colb", tag="colb")
+            for i in mine:
+                r0, nr = pieces[i][1], pieces[i][2]
+                for j in range(nr):
+                    r = r0 + j
+                    blk = a_tiles[i][:, j, col0 : col0 + K]
+                    if u == 0:
+                        plus = work.tile([P, K], F32, name="plus")
+                        nc.gpsimd.tensor_tensor(out=plus[:], in0=blk, in1=epad[:, 3 - r : 3 - r + K], op=ALU.add)
+                        blk = plus[:]
+                    nc.vector.scalar_tensor_tensor(
+                        out=colb[:, r, :],
+                        in0=blk,
+                        scalar=dinv[:, r : r + 1],
+                        in1=dj_flat,
+                        op0=ALU.mult,
+                        op1=ALU.mult,
+                    )
+            for i in mine:
+                if n_loaded < len(pieces):
+                    issue_load(n_loaded)
+                    n_loaded += 1
+
+            grp = work.tile([P, 4, P, 4], BF16, name="grp", tag="grp", align_bytes=64)
+            for i in mine:
+                r0, nr = pieces[i][1], pieces[i][2]
+                xt = ps_t.tile([P, 2, 4, P], BF16, name="xt")
+                for j in range(nr):
+                    for t in range(4):
+                        nc.tensor.transpose(xt[:, j, t, :], colb[:, r0 + j, t * P : (t + 1) * P], ident_b[:])
+                nc.scalar.copy(out=grp[:, r0 : r0 + nr, :, :], in_=xt[:, 0:nr, :, :].rearrange("q r t i -> q r i t"))
+            codes = work.tile([P, 4 * P], U32, name="codes", align_bytes=64)
+            scl = work.tile([P, 4 * P], U8, name="scl", align_bytes=64)
+            nc.vector.quantize_mx(
+                out=codes[:, 0 : rows * P].bitcast(FP8X4),
+                scales=scl[:, 0 : rows * P],
+                in_=grp[:, 0:rows, :, :].rearrange("q r i t -> q (r i t)"),
+            )
+            y_sb = ypool.tile([P, 2, rows, 256], F32, name="y_sb", tag="y_sb")
+            for r in range(rows):
+                y_ps = ps_y.tile([P, K], F32, name="y_ps")
+                nc.tensor.matmul_mx(
+                    out=y_ps[:],
+                    lhsT=codes[:, r * P : (r + 1) * P].bitcast(FP8X4),
+                    lhsT_scale=scl[:, r * P : (r + 1) * P],
+                    rhs=x_codes[:].bitcast(FP8X4),
+                    rhs_scale=x_scales[:],
+                    start=True,
+                    stop=True,
+                )
+                nc.scalar.copy(out=y_sb[:, :, r, :], in_=y_ps[:].rearrange("p (b f) -> p b f", b=2))
+            nc.scalar.dma_start(
+                out=out[:, base : base + P * rows, :].rearrange("b (p r) f -> p b (r f)", r=rows),
+                in_=y_sb[:].rearrange("p b r f -> p b (r f)"),
+            )

@@ -16,14 +16,14 @@ ACT = mybir.ActivationFunctionType
 P = 128
 N = 3584
 K = 512
-HV = 1312
-A_BUFS = 10
+CV = 3008
+A_BUFS = 9
 
 
 def tile_gcn_kernel(tc, adj, feats, batch_size, output_dim, client, out):
     nc = tc.nc
     col0 = client * K
-    cs = N - 2 * HV
+    cs = N - CV
     units = [(col0, 4), (0, 4), (512, 4), (1024, 4), (2048, 4), (2560, 4), (3072, 2), (3328, 1), (3456, 1)]
     pieces = []
     for u, (base, rows) in enumerate(units):
@@ -36,6 +36,7 @@ def tile_gcn_kernel(tc, adj, feats, batch_size, output_dim, client, out):
         work = ctx.enter_context(tc.tile_pool(name="work", bufs=2))
         small = ctx.enter_context(tc.tile_pool(name="small", bufs=4))
         ypool = ctx.enter_context(tc.tile_pool(name="ypool", bufs=3))
+        zpool = ctx.enter_context(tc.tile_pool(name="zpool", bufs=3))
         ps_t = ctx.enter_context(tc.psum_pool(name="ps_t", bufs=3))
         ps_y = ctx.enter_context(tc.psum_pool(name="ps_y", bufs=4))
         ps_d = ctx.enter_context(tc.psum_pool(name="ps_d", bufs=1))
@@ -85,12 +86,12 @@ def tile_gcn_kernel(tc, adj, feats, batch_size, output_dim, client, out):
                 r0, nr = pieces[i][1], pieces[i][2]
                 for j in range(nr):
                     r = r0 + j
-                    junk_v = work.tile([P, HV], F32, name="junk_v")
-                    nc.vector.scalar_tensor_tensor(
+                    junk_v = work.tile([P, CV], BF16, name="junk_v")
+                    nc.vector.tensor_scalar(
                         out=junk_v[:],
-                        in0=a_tiles[i][:, j, 0:HV],
-                        scalar=1.0,
-                        in1=a_tiles[i][:, j, HV : 2 * HV],
+                        in0=a_tiles[i][:, j, 0:CV],
+                        scalar1=1.0,
+                        scalar2=None,
                         op0=ALU.mult,
                         op1=ALU.add,
                         accum_out=s_v[:, r : r + 1],
@@ -98,7 +99,7 @@ def tile_gcn_kernel(tc, adj, feats, batch_size, output_dim, client, out):
                     junk_s = work.tile([P, cs], BF16, name="junk_s")
                     nc.scalar.activation(
                         out=junk_s[:],
-                        in_=a_tiles[i][:, j, 2 * HV : N],
+                        in_=a_tiles[i][:, j, CV:N],
                         func=ACT.Copy,
                         accum_out=s_s[:, r : r + 1],
                     )
@@ -127,20 +128,31 @@ def tile_gcn_kernel(tc, adj, feats, batch_size, output_dim, client, out):
             colb = work.tile([P, 4, K], BF16, name="colb", tag="colb")
             for i in mine:
                 r0, nr = pieces[i][1], pieces[i][2]
+                blk = a_tiles[i][:, 0:nr, col0 : col0 + K]
+                if u == 0:
+                    plus = zpool.tile([P, 2, K], F32, name="plus", tag="plus", bufs=2)
+                    for j in range(nr):
+                        r = r0 + j
+                        nc.gpsimd.tensor_tensor(
+                            out=plus[:, j, :], in0=blk[:, j, :], in1=epad[:, 3 - r : 3 - r + K], op=ALU.add
+                        )
+                    blk = plus[:, 0:nr, :]
+                z_t = zpool.tile([P, 2, K], F32, name="z_t")
+                nc.gpsimd.tensor_tensor(
+                    out=z_t[:, 0:nr, :],
+                    in0=blk,
+                    in1=dj_flat.unsqueeze(1).to_broadcast([P, nr, K]),
+                    op=ALU.mult,
+                )
                 for j in range(nr):
                     r = r0 + j
-                    blk = a_tiles[i][:, j, col0 : col0 + K]
-                    if u == 0:
-                        plus = work.tile([P, K], F32, name="plus")
-                        nc.gpsimd.tensor_tensor(out=plus[:], in0=blk, in1=epad[:, 3 - r : 3 - r + K], op=ALU.add)
-                        blk = plus[:]
-                    nc.vector.scalar_tensor_tensor(
+                    nc.gpsimd.tensor_scalar(
                         out=colb[:, r, :],
-                        in0=blk,
-                        scalar=dinv[:, r : r + 1],
-                        in1=dj_flat,
+                        in0=z_t[:, j, :],
+                        scalar1=dinv[:, r : r + 1],
+                        scalar2=0.0,
                         op0=ALU.mult,
-                        op1=ALU.mult,
+                        op1=ALU.add,
                     )
             for i in mine:
                 if n_loaded < len(pieces):

@@ -16,178 +16,211 @@ ACT = mybir.ActivationFunctionType
 P = 128
 N = 3584
 K = 512
-CV = 3008
-A_BUFS = 9
+HV = 1312
+A_BUFS = 8
+TAIL_V = 3
 
 
 def tile_gcn_kernel(tc, adj, feats, batch_size, output_dim, client, out):
     nc = tc.nc
     col0 = client * K
-    cs = N - CV
+    cs = N - 2 * HV
     units = [(col0, 4), (0, 4), (512, 4), (1024, 4), (2048, 4), (2560, 4), (3072, 2), (3328, 1), (3456, 1)]
     pieces = []
     for u, (base, rows) in enumerate(units):
         for r0 in range(0, rows, 2):
             pieces.append((u, r0, min(2, rows - r0)))
+    n = len(pieces)
 
     with ExitStack() as ctx:
         const = ctx.enter_context(tc.tile_pool(name="const", bufs=1))
         apool = ctx.enter_context(tc.tile_pool(name="apool", bufs=A_BUFS))
-        work = ctx.enter_context(tc.tile_pool(name="work", bufs=2))
-        small = ctx.enter_context(tc.tile_pool(name="small", bufs=4))
-        ypool = ctx.enter_context(tc.tile_pool(name="ypool", bufs=3))
-        zpool = ctx.enter_context(tc.tile_pool(name="zpool", bufs=3))
+        junk = ctx.enter_context(tc.tile_pool(name="junk", bufs=2))
+        work = ctx.enter_context(tc.tile_pool(name="work", bufs=3))
+        small = ctx.enter_context(tc.tile_pool(name="small", bufs=5))
+        ypool = ctx.enter_context(tc.tile_pool(name="ypool", bufs=1))
         ps_t = ctx.enter_context(tc.psum_pool(name="ps_t", bufs=3))
         ps_y = ctx.enter_context(tc.psum_pool(name="ps_y", bufs=4))
         ps_d = ctx.enter_context(tc.psum_pool(name="ps_d", bufs=1))
+        ctx.enter_context(tc.manual_schedule())
 
-        a_tiles = {}
-
-        def issue_load(i):
-            u, r0, nr = pieces[i]
-            base, rows = units[u]
-            a_t = apool.tile([P, 2, N], BF16, name="a_t")
-            src = adj[base : base + P * rows, :].rearrange("(p r) c -> p r c", r=rows)
-            if u == 0:
-                for j in range(nr):
-                    nc.sync.dma_start(out=a_t[:, j : j + 1, :], in_=src[:, r0 + j : r0 + j + 1, :])
-            else:
-                nc.sync.dma_start(out=a_t[:, 0:nr, :], in_=src[:, r0 : r0 + nr, :])
-            a_tiles[i] = a_t
-
-        n_loaded = min(A_BUFS, len(pieces))
-        for i in range(2):
-            issue_load(i)
-        x_raw = work.tile([P, 4, K], BF16, name="x_raw", tag="colb")
-        nc.sync.dma_start(out=x_raw[:], in_=feats.rearrange("(t q) f -> q t f", q=P))
-        for i in range(2, n_loaded):
-            issue_load(i)
+        a_t, s_v, s_s, deg, root, dinv = {}, {}, {}, {}, {}, {}
+        plus, colb, xt, grp, codes, scl, y_ps, y_sb = {}, {}, {}, {}, {}, {}, {}, {}
 
         ident_b = const.tile([P, P], BF16, name="ident_b")
-        make_identity(nc, ident_b[:])
         ident_f = const.tile([P, P], F32, name="ident_f")
-        make_identity(nc, ident_f[:])
         epad = const.tile([P, K + 4], BF16, name="epad")
-        nc.gpsimd.memset(epad[:], 0.0)
-        nc.gpsimd.tensor_copy(
-            out=epad[:, 3 : 3 + K].rearrange("p (q r) -> p q r", r=4)[:, :, 0], in_=ident_b[:]
-        )
-
+        x_raw = const.tile([P, 4, K], BF16, name="x_raw")
+        x_grp = const.tile([P, K, 4], BF16, name="x_grp", align_bytes=64)
         x_codes = const.tile([P, K], U32, name="x_codes", align_bytes=64)
         x_scales = const.tile([P, K], U8, name="x_scales", align_bytes=64)
         djb = const.tile([P, P, 4], F32, name="djb")
         dj_flat = djb[:].rearrange("m n r -> m (n r)")
 
-        for u, (base, rows) in enumerate(units):
-            mine = [i for i in range(len(pieces)) if pieces[i][0] == u]
-            s_v = small.tile([P, 4], F32, name="s_v")
-            s_s = small.tile([P, 4], F32, name="s_s")
-            for i in mine:
-                r0, nr = pieces[i][1], pieces[i][2]
-                for j in range(nr):
-                    r = r0 + j
-                    junk_v = work.tile([P, CV], BF16, name="junk_v")
-                    nc.vector.tensor_scalar(
-                        out=junk_v[:],
-                        in0=a_tiles[i][:, j, 0:CV],
-                        scalar1=1.0,
-                        scalar2=None,
-                        op0=ALU.mult,
-                        op1=ALU.add,
-                        accum_out=s_v[:, r : r + 1],
-                    )
-                    junk_s = work.tile([P, cs], BF16, name="junk_s")
-                    nc.scalar.activation(
-                        out=junk_s[:],
-                        in_=a_tiles[i][:, j, CV:N],
-                        func=ACT.Copy,
-                        accum_out=s_s[:, r : r + 1],
-                    )
-            deg = small.tile([P, 4], F32, name="deg")
-            nc.vector.scalar_tensor_tensor(
-                out=deg[:, 0:rows], in0=s_v[:, 0:rows], scalar=1.0, in1=s_s[:, 0:rows], op0=ALU.add, op1=ALU.add
-            )
-            root = small.tile([P, 4], F32, name="root")
-            nc.scalar.activation(out=root[:, 0:rows], in_=deg[:, 0:rows], func=ACT.Sqrt)
-            dinv = small.tile([P, 4], F32, name="dinv")
-            nc.vector.reciprocal(out=dinv[:, 0:rows], in_=root[:, 0:rows])
-
+        def load(k):
+            u, r0, nr = pieces[k]
+            base, rows = units[u]
+            a_t[k] = apool.tile([P, 2, N], BF16, name="a_t")
+            src = adj[base : base + P * rows, :].rearrange("(p r) c -> p r c", r=rows)
             if u == 0:
-                x_grp = work.tile([P, K, 4], BF16, name="x_grp", tag="grp", align_bytes=64)
-                nc.vector.tensor_copy(out=x_grp[:], in_=x_raw[:].rearrange("q t f -> q f t"))
-                spread = const.tile([P, 4, P], F32, name="spread")
-                nc.vector.tensor_copy(out=spread[:], in_=dinv[:].unsqueeze(2).to_broadcast([P, 4, P]))
-                dj_ps = ps_d.tile([P, 4, P], F32, name="dj_ps")
-                for r in range(4):
-                    nc.tensor.transpose(dj_ps[:, r, :], spread[:, r, :], ident_f[:])
-                nc.vector.tensor_copy(out=djb[:], in_=dj_ps[:].rearrange("m r n -> m n r"))
-                nc.vector.quantize_mx(
-                    out=x_codes[:].bitcast(FP8X4), scales=x_scales[:], in_=x_grp[:].rearrange("q f t -> q (f t)")
-                )
+                for j in range(nr):
+                    nc.sync.dma_start(out=a_t[k][:, j : j + 1, :], in_=src[:, r0 + j : r0 + j + 1, :])
+            else:
+                nc.sync.dma_start(out=a_t[k][:, 0:nr, :], in_=src[:, r0 : r0 + nr, :])
 
-            colb = work.tile([P, 4, K], BF16, name="colb", tag="colb")
-            for i in mine:
-                r0, nr = pieces[i][1], pieces[i][2]
-                blk = a_tiles[i][:, 0:nr, col0 : col0 + K]
-                if u == 0:
-                    plus = zpool.tile([P, 2, K], F32, name="plus", tag="plus", bufs=2)
-                    for j in range(nr):
-                        r = r0 + j
-                        nc.gpsimd.tensor_tensor(
-                            out=plus[:, j, :], in0=blk[:, j, :], in1=epad[:, 3 - r : 3 - r + K], op=ALU.add
-                        )
-                    blk = plus[:, 0:nr, :]
-                z_t = zpool.tile([P, 2, K], F32, name="z_t")
-                nc.gpsimd.tensor_tensor(
-                    out=z_t[:, 0:nr, :],
-                    in0=blk,
-                    in1=dj_flat.unsqueeze(1).to_broadcast([P, nr, K]),
-                    op=ALU.mult,
+        def sums(k):
+            u, r0, nr = pieces[k]
+            s_v[k] = small.tile([P, 2], F32, name="s_v")
+            s_s[k] = small.tile([P, 2], F32, name="s_s")
+            for j in range(nr):
+                junk_v = junk.tile([P, HV], F32, name="junk_v")
+                nc.vector.scalar_tensor_tensor(
+                    out=junk_v[:],
+                    in0=a_t[k][:, j, 0:HV],
+                    scalar=1.0,
+                    in1=a_t[k][:, j, HV : 2 * HV],
+                    op0=ALU.mult,
+                    op1=ALU.add,
+                    accum_out=s_v[k][:, j : j + 1],
                 )
+                junk_s = junk.tile([P, cs], BF16, name="junk_s")
+                nc.scalar.activation(
+                    out=junk_s[:], in_=a_t[k][:, j, 2 * HV : N], func=ACT.Copy, accum_out=s_s[k][:, j : j + 1]
+                )
+            if u == 0:
+                plus[k] = const.tile([P, 2, K], F32, name="plus%d" % k)
                 for j in range(nr):
                     r = r0 + j
-                    nc.gpsimd.tensor_scalar(
-                        out=colb[:, r, :],
-                        in0=z_t[:, j, :],
-                        scalar1=dinv[:, r : r + 1],
-                        scalar2=0.0,
-                        op0=ALU.mult,
-                        op1=ALU.add,
+                    nc.gpsimd.tensor_tensor(
+                        out=plus[k][:, j, :],
+                        in0=a_t[k][:, j, col0 : col0 + K],
+                        in1=epad[:, 3 - r : 3 - r + K],
+                        op=ALU.add,
                     )
-            for i in mine:
-                if n_loaded < len(pieces):
-                    issue_load(n_loaded)
-                    n_loaded += 1
 
-            grp = work.tile([P, 4, P, 4], BF16, name="grp", tag="grp", align_bytes=64)
-            for i in mine:
-                r0, nr = pieces[i][1], pieces[i][2]
-                xt = ps_t.tile([P, 2, 4, P], BF16, name="xt")
-                for j in range(nr):
-                    for t in range(4):
-                        nc.tensor.transpose(xt[:, j, t, :], colb[:, r0 + j, t * P : (t + 1) * P], ident_b[:])
-                nc.scalar.copy(out=grp[:, r0 : r0 + nr, :, :], in_=xt[:, 0:nr, :, :].rearrange("q r t i -> q r i t"))
-            codes = work.tile([P, 4 * P], U32, name="codes", align_bytes=64)
-            scl = work.tile([P, 4 * P], U8, name="scl", align_bytes=64)
-            nc.vector.quantize_mx(
-                out=codes[:, 0 : rows * P].bitcast(FP8X4),
-                scales=scl[:, 0 : rows * P],
-                in_=grp[:, 0:rows, :, :].rearrange("q r i t -> q (r i t)"),
+        def rsqrt(k):
+            nr = pieces[k][2]
+            deg[k] = small.tile([P, 2], F32, name="deg")
+            root[k] = small.tile([P, 2], F32, name="root")
+            if pieces[k][0] == 0:
+                dinv[k] = dinv0[:, 2 * k : 2 * k + 2]
+            else:
+                dinv[k] = small.tile([P, 2], F32, name="dinv")
+            nc.gpsimd.tensor_tensor(out=deg[k][:, 0:nr], in0=s_v[k][:, 0:nr], in1=s_s[k][:, 0:nr], op=ALU.add)
+            nc.gpsimd.tensor_scalar(
+                out=root[k][:, 0:nr], in0=deg[k][:, 0:nr], scalar1=1.0, scalar2=1.0, op0=ALU.add, op1=ALU.mult
             )
-            y_sb = ypool.tile([P, 2, rows, 256], F32, name="y_sb", tag="y_sb")
-            for r in range(rows):
-                y_ps = ps_y.tile([P, K], F32, name="y_ps")
+            nc.gpsimd.tensor_tensor(out=dinv[k][:, 0:nr], in0=root[k][:, 0:nr], in1=mhalf[:, 0:nr], op=ALU.pow)
+
+        def scale_transpose(k):
+            u, r0, nr = pieces[k]
+            colb[k] = work.tile([P, 2, K], BF16, name="colb")
+            xt[k] = ps_t.tile([P, 2, 4, P], BF16, name="xt")
+            for j in range(nr):
+                blk = plus[k][:, j, :] if u == 0 else a_t[k][:, j, col0 : col0 + K]
+                nc.vector.scalar_tensor_tensor(
+                    out=colb[k][:, j, :],
+                    in0=blk,
+                    scalar=dinv[k][:, j : j + 1],
+                    in1=dj_flat,
+                    op0=ALU.mult,
+                    op1=ALU.mult,
+                )
+                for t in range(4):
+                    nc.tensor.transpose(xt[k][:, j, t, :], colb[k][:, j, t * P : (t + 1) * P], ident_b[:])
+
+        def regroup(k):
+            nr = pieces[k][2]
+            grp[k] = work.tile([P, 2, P, 4], BF16, name="grp", align_bytes=64)
+            nc.scalar.copy(out=grp[k][:, 0:nr, :, :], in_=xt[k][:, 0:nr, :, :].rearrange("q r t i -> q r i t"))
+
+        def quant_mm(k):
+            nr = pieces[k][2]
+            codes[k] = work.tile([P, 2 * P], U32, name="codes", align_bytes=64)
+            scl[k] = work.tile([P, 2 * P], U8, name="scl", align_bytes=64)
+            nc.vector.quantize_mx(
+                out=codes[k][:, 0 : nr * P].bitcast(FP8X4),
+                scales=scl[k][:, 0 : nr * P],
+                in_=grp[k][:, 0:nr, :, :].rearrange("q r i t -> q (r i t)"),
+            )
+            for j in range(nr):
+                y_ps[(k, j)] = ps_y.tile([P, K], F32, name="y_ps")
                 nc.tensor.matmul_mx(
-                    out=y_ps[:],
-                    lhsT=codes[:, r * P : (r + 1) * P].bitcast(FP8X4),
-                    lhsT_scale=scl[:, r * P : (r + 1) * P],
+                    out=y_ps[(k, j)][:],
+                    lhsT=codes[k][:, j * P : (j + 1) * P].bitcast(FP8X4),
+                    lhsT_scale=scl[k][:, j * P : (j + 1) * P],
                     rhs=x_codes[:].bitcast(FP8X4),
                     rhs_scale=x_scales[:],
                     start=True,
                     stop=True,
                 )
-                nc.scalar.copy(out=y_sb[:, :, r, :], in_=y_ps[:].rearrange("p (b f) -> p b f", b=2))
-            nc.scalar.dma_start(
-                out=out[:, base : base + P * rows, :].rearrange("b (p r) f -> p b (r f)", r=rows),
-                in_=y_sb[:].rearrange("p b r f -> p b (r f)"),
+
+        def leave(k):
+            u, r0, nr = pieces[k]
+            base, rows = units[u]
+            if r0 == 0:
+                y_sb[u] = ypool.tile([P, 2, rows, 256], F32, name="y_sb%d" % u)
+            for j in range(nr):
+                dst = y_sb[u][:, :, r0 + j, :]
+                src = y_ps[(k, j)][:].rearrange("p (b f) -> p b f", b=2)
+                if k >= n - TAIL_V and (k + j) % 2 == 1:
+                    nc.vector.tensor_copy(out=dst, in_=src)
+                else:
+                    nc.scalar.copy(out=dst, in_=src)
+            if r0 + nr == rows:
+                nc.scalar.dma_start(
+                    out=out[:, base : base + P * rows, :].rearrange("b (p r) f -> p b (r f)", r=rows),
+                    in_=y_sb[u][:].rearrange("p b r f -> p b (r f)"),
+                )
+
+        load(0)
+        load(1)
+        nc.sync.dma_start(out=x_raw[:], in_=feats.rearrange("(t q) f -> q t f", q=P))
+        for k in range(2, A_BUFS):
+            load(k)
+        make_identity(nc, ident_b[:])
+        nc.gpsimd.memset(epad[:], 0.0)
+        nc.gpsimd.tensor_copy(
+            out=epad[:, 3 : 3 + K].rearrange("p (q r) -> p q r", r=4)[:, :, 0], in_=ident_b[:]
+        )
+        make_identity(nc, ident_f[:])
+        mhalf = const.tile([P, 2], F32, name="mhalf")
+        nc.gpsimd.memset(mhalf[:], -0.5)
+        dinv0 = const.tile([P, 4], F32, name="dinv0")
+
+        for k in range(2):
+            sums(k)
+            rsqrt(k)
+        dj_ps = ps_d.tile([P, 4, P], F32, name="dj_ps")
+        for r in range(4):
+            nc.tensor.matmul(
+                out=dj_ps[:, r, :],
+                lhsT=dinv0[:, r : r + 1].to_broadcast([P, P]),
+                rhs=ident_f[:],
+                start=True,
+                stop=True,
             )
+        nc.gpsimd.tensor_scalar(
+            out=x_grp[:], in0=x_raw[:].rearrange("q t f -> q f t"), scalar1=1.0, scalar2=0.0, op0=ALU.mult, op1=ALU.add
+        )
+        nc.vector.tensor_copy(out=djb[:], in_=dj_ps[:].rearrange("m r n -> m n r"))
+        scale_transpose(0)
+        load(A_BUFS)
+        nc.vector.quantize_mx(
+            out=x_codes[:].bitcast(FP8X4), scales=x_scales[:], in_=x_grp[:].rearrange("q f t -> q (f t)")
+        )
+
+        for k in range(2, n + 3):
+            if k < n:
+                sums(k)
+                rsqrt(k)
+            if k - 2 < n:
+                regroup(k - 2)
+            if k - 1 < n:
+                scale_transpose(k - 1)
+                if k - 1 + A_BUFS < n:
+                    load(k - 1 + A_BUFS)
+            if k - 2 < n:
+                quant_mm(k - 2)
+            if k >= 3:
+                leave(k - 3)

@@ -16,7 +16,7 @@ ACT = mybir.ActivationFunctionType
 P = 128
 N = 3584
 K = 512
-HV = 1312
+HV = 1536
 A_BUFS = 8
 TAIL_V = 3
 

@@ -16,7 +16,7 @@ ACT = mybir.ActivationFunctionType
 P = 128
 N = 3584
 K = 512
-HV = 1536
+HV = 1280
 A_BUFS = 8
 TAIL_V = 3
 
@@ -44,7 +44,7 @@ def tile_gcn_kernel(tc, adj, feats, batch_size, output_dim, client, out):
         ps_d = ctx.enter_context(tc.psum_pool(name="ps_d", bufs=1))
         ctx.enter_context(tc.manual_schedule())
 
-        a_t, s_v, s_s, deg, root, dinv = {}, {}, {}, {}, {}, {}
+        a_t, s_v, s_s, dinv = {}, {}, {}, {}
         plus, colb, xt, grp, codes, scl, y_ps, y_sb = {}, {}, {}, {}, {}, {}, {}, {}
 
         ident_b = const.tile([P, P], BF16, name="ident_b")
@@ -85,32 +85,38 @@ def tile_gcn_kernel(tc, adj, feats, batch_size, output_dim, client, out):
                 )
                 junk_s = junk.tile([P, cs], BF16, name="junk_s")
                 nc.scalar.activation(
-                    out=junk_s[:], in_=a_t[k][:, j, 2 * HV : N], func=ACT.Copy, accum_out=s_s[k][:, j : j + 1]
+                    out=junk_s[:],
+                    in_=a_t[k][:, j, 2 * HV : N],
+                    func=ACT.Copy,
+                    bias=1.0 / cs,
+                    accum_out=s_s[k][:, j : j + 1],
                 )
-            if u == 0:
-                plus[k] = const.tile([P, 2, K], F32, name="plus%d" % k)
-                for j in range(nr):
-                    r = r0 + j
-                    nc.gpsimd.tensor_tensor(
-                        out=plus[k][:, j, :],
-                        in0=a_t[k][:, j, col0 : col0 + K],
-                        in1=epad[:, 3 - r : 3 - r + K],
-                        op=ALU.add,
-                    )
+
+        def add_identity(k):
+            u, r0, nr = pieces[k]
+            plus[k] = const.tile([P, 2, K], F32, name="plus%d" % k)
+            for j in range(nr):
+                r = r0 + j
+                nc.vector.tensor_tensor(
+                    out=plus[k][:, j, :],
+                    in0=a_t[k][:, j, col0 : col0 + K],
+                    in1=epad[:, 3 - r : 3 - r + K],
+                    op=ALU.add,
+                )
 
         def rsqrt(k):
             nr = pieces[k][2]
-            deg[k] = small.tile([P, 2], F32, name="deg")
-            root[k] = small.tile([P, 2], F32, name="root")
             if pieces[k][0] == 0:
                 dinv[k] = dinv0[:, 2 * k : 2 * k + 2]
             else:
                 dinv[k] = small.tile([P, 2], F32, name="dinv")
-            nc.gpsimd.tensor_tensor(out=deg[k][:, 0:nr], in0=s_v[k][:, 0:nr], in1=s_s[k][:, 0:nr], op=ALU.add)
-            nc.gpsimd.tensor_scalar(
-                out=root[k][:, 0:nr], in0=deg[k][:, 0:nr], scalar1=1.0, scalar2=1.0, op0=ALU.add, op1=ALU.mult
-            )
-            nc.gpsimd.tensor_tensor(out=dinv[k][:, 0:nr], in0=root[k][:, 0:nr], in1=mhalf[:, 0:nr], op=ALU.pow)
+            for j in range(nr):
+                nc.scalar.activation(
+                    out=dinv[k][:, j : j + 1],
+                    in_=s_v[k][:, j : j + 1],
+                    func=ACT.Abs_reciprocal_sqrt,
+                    bias=s_s[k][:, j : j + 1],
+                )
 
         def scale_transpose(k):
             u, r0, nr = pieces[k]
@@ -184,8 +190,9 @@ def tile_gcn_kernel(tc, adj, feats, batch_size, output_dim, client, out):
             out=epad[:, 3 : 3 + K].rearrange("p (q r) -> p q r", r=4)[:, :, 0], in_=ident_b[:]
         )
         make_identity(nc, ident_f[:])
-        mhalf = const.tile([P, 2], F32, name="mhalf")
-        nc.gpsimd.memset(mhalf[:], -0.5)
+        warm = const.tile([P, 1], F32, name="warm")
+        nc.vector.memset(warm[:], 1.0)
+        nc.scalar.activation(out=warm[:], in_=warm[:], func=ACT.Abs_reciprocal_sqrt)
         dinv0 = const.tile([P, 4], F32, name="dinv0")
 
         for k in range(2):
@@ -200,9 +207,9 @@ def tile_gcn_kernel(tc, adj, feats, batch_size, output_dim, client, out):
                 start=True,
                 stop=True,
             )
-        nc.gpsimd.tensor_scalar(
-            out=x_grp[:], in0=x_raw[:].rearrange("q t f -> q f t"), scalar1=1.0, scalar2=0.0, op0=ALU.mult, op1=ALU.add
-        )
+        nc.scalar.copy(out=x_grp[:], in_=x_raw[:].rearrange("q t f -> q f t"))
+        add_identity(0)
+        add_identity(1)
         nc.vector.tensor_copy(out=djb[:], in_=dj_ps[:].rearrange("m r n -> m n r"))
         scale_transpose(0)
         load(A_BUFS)
@@ -213,9 +220,10 @@ def tile_gcn_kernel(tc, adj, feats, batch_size, output_dim, client, out):
         for k in range(2, n + 3):
             if k < n:
                 sums(k)
-                rsqrt(k)
             if k - 2 < n:
                 regroup(k - 2)
+            if k < n:
+                rsqrt(k)
             if k - 1 < n:
                 scale_transpose(k - 1)
                 if k - 1 + A_BUFS < n:

@@ -16,15 +16,14 @@ ACT = mybir.ActivationFunctionType
 P = 128
 N = 3584
 K = 512
-HV = 1280
-A_BUFS = 8
+CS = 2048
+A_BUFS = 7
 TAIL_V = 3
 
 
 def tile_gcn_kernel(tc, adj, feats, batch_size, output_dim, client, out):
     nc = tc.nc
     col0 = client * K
-    cs = N - 2 * HV
     units = [(col0, 4), (0, 4), (512, 4), (1024, 4), (2048, 4), (2560, 4), (3072, 2), (3328, 1), (3456, 1)]
     pieces = []
     for u, (base, rows) in enumerate(units):
@@ -73,23 +72,25 @@ def tile_gcn_kernel(tc, adj, feats, batch_size, output_dim, client, out):
             s_v[k] = small.tile([P, 2], F32, name="s_v")
             s_s[k] = small.tile([P, 2], F32, name="s_s")
             for j in range(nr):
-                junk_v = junk.tile([P, HV], F32, name="junk_v")
+                half = (N - j * CS) // 2
+                junk_v = junk.tile([P, N // 2], F32, name="junk_v")
                 nc.vector.scalar_tensor_tensor(
-                    out=junk_v[:],
-                    in0=a_t[k][:, j, 0:HV],
+                    out=junk_v[:, 0:half],
+                    in0=a_t[k][:, j, 0:half],
                     scalar=1.0,
-                    in1=a_t[k][:, j, HV : 2 * HV],
+                    in1=a_t[k][:, j, half : 2 * half],
                     op0=ALU.mult,
                     op1=ALU.add,
                     accum_out=s_v[k][:, j : j + 1],
                 )
-                junk_s = junk.tile([P, cs], BF16, name="junk_s")
+            if nr == 2:
+                junk_s = junk.tile([P, CS], BF16, name="junk_s")
                 nc.scalar.activation(
                     out=junk_s[:],
-                    in_=a_t[k][:, j, 2 * HV : N],
+                    in_=a_t[k][:, 1, N - CS : N],
                     func=ACT.Copy,
-                    bias=1.0 / cs,
-                    accum_out=s_s[k][:, j : j + 1],
+                    bias=1.0 / CS,
+                    accum_out=s_s[k][:, 0:1],
                 )
 
         def add_identity(k):
@@ -115,7 +116,7 @@ def tile_gcn_kernel(tc, adj, feats, batch_size, output_dim, client, out):
                     out=dinv[k][:, j : j + 1],
                     in_=s_v[k][:, j : j + 1],
                     func=ACT.Abs_reciprocal_sqrt,
-                    bias=s_s[k][:, j : j + 1],
+                    bias=(1.0 if j == 0 else s_s[k][:, 0:1]),
                 )
 
         def scale_transpose(k):
@@ -174,7 +175,7 @@ def tile_gcn_kernel(tc, adj, feats, batch_size, output_dim, client, out):
                 else:
                     nc.scalar.copy(out=dst, in_=src)
             if r0 + nr == rows:
-                nc.scalar.dma_start(
+                nc.sync.dma_start(
                     out=out[:, base : base + P * rows, :].rearrange("b (p r) f -> p b (r f)", r=rows),
                     in_=y_sb[u][:].rearrange("p b r f -> p b (r f)"),
                 )

@@ -16,7 +16,8 @@ ACT = mybir.ActivationFunctionType
 P = 128
 N = 3584
 K = 512
-CS = 2048
+CS = 1792
+CH = 1536
 A_BUFS = 7
 TAIL_V = 3
 
@@ -93,24 +94,47 @@ def tile_gcn_kernel(tc, adj, feats, batch_size, output_dim, client, out):
                     accum_out=s_s[k][:, 0:1],
                 )
 
-        def add_identity(k):
-            u, r0, nr = pieces[k]
-            plus[k] = const.tile([P, 2, K], F32, name="plus%d" % k)
-            for j in range(nr):
-                r = r0 + j
-                nc.vector.tensor_tensor(
-                    out=plus[k][:, j, :],
-                    in0=a_t[k][:, j, col0 : col0 + K],
-                    in1=epad[:, 3 - r : 3 - r + K],
-                    op=ALU.add,
-                )
+        def head_row(k, j):
+            r = 2 * k + j
+            half = (N - CH) // 2
+            junk_v = junk.tile([P, N // 2], F32, name="junk_v")
+            nc.vector.scalar_tensor_tensor(
+                out=junk_v[:, 0:half],
+                in0=a_t[k][:, j, 0:half],
+                scalar=1.0,
+                in1=a_t[k][:, j, half : 2 * half],
+                op0=ALU.mult,
+                op1=ALU.add,
+                accum_out=s_v0[:, r : r + 1],
+            )
+            junk_s = junk.tile([P, CS], BF16, name="junk_s")
+            nc.scalar.activation(
+                out=junk_s[:, 0:CH],
+                in_=a_t[k][:, j, N - CH : N],
+                func=ACT.Copy,
+                bias=1.0 / CH,
+                accum_out=s_s0[:, r : r + 1],
+            )
+            nc.vector.tensor_tensor(
+                out=plus[k][:, j, :], in0=a_t[k][:, j, col0 : col0 + K], in1=epad[:, 3 - r : 3 - r + K], op=ALU.add
+            )
+            nc.scalar.activation(
+                out=dinv0[:, r : r + 1],
+                in_=s_v0[:, r : r + 1],
+                func=ACT.Abs_reciprocal_sqrt,
+                bias=s_s0[:, r : r + 1],
+            )
+            nc.tensor.matmul(
+                out=dj_ps[:, r, :],
+                lhsT=dinv0[:, r : r + 1].to_broadcast([P, P]),
+                rhs=ident_f[:],
+                start=True,
+                stop=True,
+            )
 
         def rsqrt(k):
             nr = pieces[k][2]
-            if pieces[k][0] == 0:
-                dinv[k] = dinv0[:, 2 * k : 2 * k + 2]
-            else:
-                dinv[k] = small.tile([P, 2], F32, name="dinv")
+            dinv[k] = small.tile([P, 2], F32, name="dinv")
             for j in range(nr):
                 nc.scalar.activation(
                     out=dinv[k][:, j : j + 1],
@@ -196,24 +220,19 @@ def tile_gcn_kernel(tc, adj, feats, batch_size, output_dim, client, out):
         nc.scalar.activation(out=warm[:], in_=warm[:], func=ACT.Abs_reciprocal_sqrt)
         dinv0 = const.tile([P, 4], F32, name="dinv0")
 
-        for k in range(2):
-            sums(k)
-            rsqrt(k)
+        s_v0 = const.tile([P, 4], F32, name="s_v0")
+        s_s0 = const.tile([P, 4], F32, name="s_s0")
         dj_ps = ps_d.tile([P, 4, P], F32, name="dj_ps")
-        for r in range(4):
-            nc.tensor.matmul(
-                out=dj_ps[:, r, :],
-                lhsT=dinv0[:, r : r + 1].to_broadcast([P, P]),
-                rhs=ident_f[:],
-                start=True,
-                stop=True,
-            )
+        for k in range(2):
+            plus[k] = const.tile([P, 2, K], F32, name="plus%d" % k)
+            dinv[k] = dinv0[:, 2 * k : 2 * k + 2]
+            for j in range(2):
+                head_row(k, j)
         nc.scalar.copy(out=x_grp[:], in_=x_raw[:].rearrange("q t f -> q f t"))
-        add_identity(0)
-        add_identity(1)
         nc.vector.tensor_copy(out=djb[:], in_=dj_ps[:].rearrange("m r n -> m n r"))
-        scale_transpose(0)
-        load(A_BUFS)
+        for k in range(2):
+            scale_transpose(k)
+            load(A_BUFS + k)
         nc.vector.quantize_mx(
             out=x_codes[:].bitcast(FP8X4), scales=x_scales[:], in_=x_grp[:].rearrange("q f t -> q (f t)")
         )
@@ -225,7 +244,7 @@ def tile_gcn_kernel(tc, adj, feats, batch_size, output_dim, client, out):
                 regroup(k - 2)
             if k < n:
                 rsqrt(k)
-            if k - 1 < n:
+            if 2 <= k - 1 < n:
                 scale_transpose(k - 1)
                 if k - 1 + A_BUFS < n:
                     load(k - 1 + A_BUFS)

from contextlib import ExitStack

import concourse.mybir as mybir
from concourse.masks import make_identity

FLOPS = 2 * 3584 * 512 * 512

BF16 = mybir.dt.bfloat16
F32 = mybir.dt.float32
U32 = mybir.dt.uint32
U8 = mybir.dt.uint8
FP8X4 = mybir.dt.float8_e4m3fn_x4
ALU = mybir.AluOpType
ACT = mybir.ActivationFunctionType

P = 128
N = 3584
K = 512
CS = 1792
CH = 1536
A_BUFS = 7
TAIL_V = 3


def tile_gcn_kernel(tc, adj, feats, batch_size, output_dim, client, out):
    nc = tc.nc
    col0 = client * K
    units = [(col0, 4), (0, 4), (512, 4), (1024, 4), (2048, 4), (2560, 4), (3072, 2), (3328, 1), (3456, 1)]
    pieces = []
    for u, (base, rows) in enumerate(units):
        for r0 in range(0, rows, 2):
            pieces.append((u, r0, min(2, rows - r0)))
    n = len(pieces)

    with ExitStack() as ctx:
        const = ctx.enter_context(tc.tile_pool(name="const", bufs=1))
        apool = ctx.enter_context(tc.tile_pool(name="apool", bufs=A_BUFS))
        junk = ctx.enter_context(tc.tile_pool(name="junk", bufs=2))
        work = ctx.enter_context(tc.tile_pool(name="work", bufs=3))
        small = ctx.enter_context(tc.tile_pool(name="small", bufs=5))
        ypool = ctx.enter_context(tc.tile_pool(name="ypool", bufs=1))
        ps_t = ctx.enter_context(tc.psum_pool(name="ps_t", bufs=3))
        ps_y = ctx.enter_context(tc.psum_pool(name="ps_y", bufs=4))
        ps_d = ctx.enter_context(tc.psum_pool(name="ps_d", bufs=1))
        ctx.enter_context(tc.manual_schedule())

        a_t, s_v, s_s, dinv = {}, {}, {}, {}
        plus, colb, xt, grp, codes, scl, y_ps, y_sb = {}, {}, {}, {}, {}, {}, {}, {}

        ident_b = const.tile([P, P], BF16, name="ident_b")
        ident_f = const.tile([P, P], F32, name="ident_f")
        epad = const.tile([P, K + 4], BF16, name="epad")
        x_raw = const.tile([P, 4, K], BF16, name="x_raw")
        x_grp = const.tile([P, K, 4], BF16, name="x_grp", align_bytes=64)
        x_codes = const.tile([P, K], U32, name="x_codes", align_bytes=64)
        x_scales = const.tile([P, K], U8, name="x_scales", align_bytes=64)
        djb = const.tile([P, P, 4], F32, name="djb")
        dj_flat = djb[:].rearrange("m n r -> m (n r)")

        def load(k):
            u, r0, nr = pieces[k]
            base, rows = units[u]
            a_t[k] = apool.tile([P, 2, N], BF16, name="a_t")
            src = adj[base : base + P * rows, :].rearrange("(p r) c -> p r c", r=rows)
            if u == 0:
                for j in range(nr):
                    nc.sync.dma_start(out=a_t[k][:, j : j + 1, :], in_=src[:, r0 + j : r0 + j + 1, :])
            else:
                nc.sync.dma_start(out=a_t[k][:, 0:nr, :], in_=src[:, r0 : r0 + nr, :])

        def sums(k):
            u, r0, nr = pieces[k]
            s_v[k] = small.tile([P, 2], F32, name="s_v")
            s_s[k] = small.tile([P, 2], F32, name="s_s")
            for j in range(nr):
                half = (N - j * CS) // 2
                junk_v = junk.tile([P, N // 2], F32, name="junk_v")
                nc.vector.scalar_tensor_tensor(
                    out=junk_v[:, 0:half],
                    in0=a_t[k][:, j, 0:half],
                    scalar=1.0,
                    in1=a_t[k][:, j, half : 2 * half],
                    op0=ALU.mult,
                    op1=ALU.add,
                    accum_out=s_v[k][:, j : j + 1],
                )
            if nr == 2:
                junk_s = junk.tile([P, CS], BF16, name="junk_s")
                nc.scalar.activation(
                    out=junk_s[:],
                    in_=a_t[k][:, 1, N - CS : N],
                    func=ACT.Copy,
                    bias=1.0 / CS,
                    accum_out=s_s[k][:, 0:1],
                )

        def head_row(k, j):
            r = 2 * k + j
            half = (N - CH) // 2
            junk_v = junk.tile([P, N // 2], F32, name="junk_v")
            nc.vector.scalar_tensor_tensor(
                out=junk_v[:, 0:half],
                in0=a_t[k][:, j, 0:half],
                scalar=1.0,
                in1=a_t[k][:, j, half : 2 * half],
                op0=ALU.mult,
                op1=ALU.add,
                accum_out=s_v0[:, r : r + 1],
            )
            junk_s = junk.tile([P, CS], BF16, name="junk_s")
            nc.scalar.activation(
                out=junk_s[:, 0:CH],
                in_=a_t[k][:, j, N - CH : N],
                func=ACT.Copy,
                bias=1.0 / CH,
                accum_out=s_s0[:, r : r + 1],
            )
            nc.vector.tensor_tensor(
                out=plus[k][:, j, :], in0=a_t[k][:, j, col0 : col0 + K], in1=epad[:, 3 - r : 3 - r + K], op=ALU.add
            )
            nc.scalar.activation(
                out=dinv0[:, r : r + 1],
                in_=s_v0[:, r : r + 1],
                func=ACT.Abs_reciprocal_sqrt,
                bias=s_s0[:, r : r + 1],
            )
            nc.tensor.matmul(
                out=dj_ps[:, r, :],
                lhsT=dinv0[:, r : r + 1].to_broadcast([P, P]),
                rhs=ident_f[:],
                start=True,
                stop=True,
            )

        def rsqrt(k):
            nr = pieces[k][2]
            dinv[k] = small.tile([P, 2], F32, name="dinv")
            for j in range(nr):
                nc.scalar.activation(
                    out=dinv[k][:, j : j + 1],
                    in_=s_v[k][:, j : j + 1],
                    func=ACT.Abs_reciprocal_sqrt,
                    bias=(1.0 if j == 0 else s_s[k][:, 0:1]),
                )

        def scale_transpose(k):
            u, r0, nr = pieces[k]
            colb[k] = work.tile([P, 2, K], BF16, name="colb")
            xt[k] = ps_t.tile([P, 2, 4, P], BF16, name="xt")
            for j in range(nr):
                blk = plus[k][:, j, :] if u == 0 else a_t[k][:, j, col0 : col0 + K]
                nc.vector.scalar_tensor_tensor(
                    out=colb[k][:, j, :],
                    in0=blk,
                    scalar=dinv[k][:, j : j + 1],
                    in1=dj_flat,
                    op0=ALU.mult,
                    op1=ALU.mult,
                )
                for t in range(4):
                    nc.tensor.transpose(xt[k][:, j, t, :], colb[k][:, j, t * P : (t + 1) * P], ident_b[:])

        def regroup(k):
            nr = pieces[k][2]
            grp[k] = work.tile([P, 2, P, 4], BF16, name="grp", align_bytes=64)
            nc.scalar.copy(out=grp[k][:, 0:nr, :, :], in_=xt[k][:, 0:nr, :, :].rearrange("q r t i -> q r i t"))

        def quant_mm(k):
            nr = pieces[k][2]
            codes[k] = work.tile([P, 2 * P], U32, name="codes", align_bytes=64)
            scl[k] = work.tile([P, 2 * P], U8, name="scl", align_bytes=64)
            nc.vector.quantize_mx(
                out=codes[k][:, 0 : nr * P].bitcast(FP8X4),
                scales=scl[k][:, 0 : nr * P],
                in_=grp[k][:, 0:nr, :, :].rearrange("q r i t -> q (r i t)"),
            )
            for j in range(nr):
                y_ps[(k, j)] = ps_y.tile([P, K], F32, name="y_ps")
                nc.tensor.matmul_mx(
                    out=y_ps[(k, j)][:],
                    lhsT=codes[k][:, j * P : (j + 1) * P].bitcast(FP8X4),
                    lhsT_scale=scl[k][:, j * P : (j + 1) * P],
                    rhs=x_codes[:].bitcast(FP8X4),
                    rhs_scale=x_scales[:],
                    start=True,
                    stop=True,
                )

        def leave(k):
            u, r0, nr = pieces[k]
            base, rows = units[u]
            if r0 == 0:
                y_sb[u] = ypool.tile([P, 2, rows, 256], F32, name="y_sb%d" % u)
            for j in range(nr):
                dst = y_sb[u][:, :, r0 + j, :]
                src = y_ps[(k, j)][:].rearrange("p (b f) -> p b f", b=2)
                if k >= n - TAIL_V and (k + j) % 2 == 1:
                    nc.vector.tensor_copy(out=dst, in_=src)
                else:
                    nc.scalar.copy(out=dst, in_=src)
            if r0 + nr == rows:
                nc.sync.dma_start(
                    out=out[:, base : base + P * rows, :].rearrange("b (p r) f -> p b (r f)", r=rows),
                    in_=y_sb[u][:].rearrange("p b r f -> p b (r f)"),
                )

        load(0)
        load(1)
        nc.sync.dma_start(out=x_raw[:], in_=feats.rearrange("(t q) f -> q t f", q=P))
        for k in range(2, A_BUFS):
            load(k)
        make_identity(nc, ident_b[:])
        nc.gpsimd.memset(epad[:], 0.0)
        nc.gpsimd.tensor_copy(
            out=epad[:, 3 : 3 + K].rearrange("p (q r) -> p q r", r=4)[:, :, 0], in_=ident_b[:]
        )
        make_identity(nc, ident_f[:])
        warm = const.tile([P, 1], F32, name="warm")
        nc.vector.memset(warm[:], 1.0)
        nc.scalar.activation(out=warm[:], in_=warm[:], func=ACT.Abs_reciprocal_sqrt)
        dinv0 = const.tile([P, 4], F32, name="dinv0")

        s_v0 = const.tile([P, 4], F32, name="s_v0")
        s_s0 = const.tile([P, 4], F32, name="s_s0")
        dj_ps = ps_d.tile([P, 4, P], F32, name="dj_ps")
        for k in range(2):
            plus[k] = const.tile([P, 2, K], F32, name="plus%d" % k)
            dinv[k] = dinv0[:, 2 * k : 2 * k + 2]
            for j in range(2):
                head_row(k, j)
        nc.scalar.copy(out=x_grp[:], in_=x_raw[:].rearrange("q t f -> q f t"))
        nc.vector.tensor_copy(out=djb[:], in_=dj_ps[:].rearrange("m r n -> m n r"))
        for k in range(2):
            scale_transpose(k)
            load(A_BUFS + k)
        nc.vector.quantize_mx(
            out=x_codes[:].bitcast(FP8X4), scales=x_scales[:], in_=x_grp[:].rearrange("q f t -> q (f t)")
        )

        for k in range(2, n + 3):
            if k < n:
                sums(k)
            if k - 2 < n:
                regroup(k - 2)
            if k < n:
                rsqrt(k)
            if 2 <= k - 1 < n:
                scale_transpose(k - 1)
                if k - 1 + A_BUFS < n:
                    load(k - 1 + A_BUFS)
            if k - 2 < n:
                quant_mm(k - 2)
            if k >= 3:
                leave(k - 3)
